import numpy as np
import ml_dtypes


BF16 = ml_dtypes.bfloat16


def bf(x):
    return np.asarray(x, np.float32).astype(BF16)


def f64(x):
    return np.asarray(x).astype(np.float64)


E2M1 = np.array([0.0, 0.5, 1.0, 1.5, 2.0, 3.0, 4.0, 6.0, -0.0, -0.5, -1.0, -1.5, -2.0, -3.0, -4.0, -6.0])


def pack_weight(w, fmt):
    k, n = w.shape
    w = f64(bf(w)).reshape(k // 32, 32, n)
    amax = np.abs(w).max(1)
    if fmt == "e4m3":
        byte = np.frexp(amax)[1] - 1 + 127 - 7
    else:
        mant, ex = np.frexp(amax / 6.0)
        byte = np.where(mant > 0.5, ex, ex - 1) + 127
    byte = np.clip(np.where(amax > 0, byte, 1), 1, 254)
    scaled = (w * np.exp2(127.0 - byte)[:, None, :]).reshape(k, n).astype(np.float32)
    by_word = np.ascontiguousarray(scaled.reshape(k // 512, 128, 4, n).transpose(0, 1, 3, 2))
    if fmt == "e4m3":
        words = by_word.astype(ml_dtypes.float8_e4m3fn).view(np.uint8)
    else:
        c = by_word.astype(ml_dtypes.float4_e2m1fn).view(np.uint8) & 0xF
        words = c[..., 0::2] | (c[..., 1::2] << 4)
    return np.ascontiguousarray(words), np.ascontiguousarray(byte.astype(np.uint8).reshape(k // 512, 16, n))


def unpack_weight(words, scales, fmt):
    g, p, n, _ = words.shape
    if fmt == "e4m3":
        vals = np.ascontiguousarray(words).view(ml_dtypes.float8_e4m3fn).astype(np.float64)
    else:
        nib = np.empty((g, p, n, 4), np.uint8)
        nib[..., 0::2] = words & 0xF
        nib[..., 1::2] = words >> 4
        vals = E2M1[nib]
    vals = vals * np.repeat(np.exp2(scales.astype(np.float64) - 127.0), 8, axis=1)[..., None]
    return vals.transpose(0, 1, 3, 2).reshape(g * 512, n)

def pack4(w):
    words, scales = pack_weight(w, "e2m1")
    return words.reshape(words.shape[0], 128, -1), scales


def unpack4(words, scales):
    return unpack_weight(words.reshape(words.shape[0], 128, -1, 2), scales, "e2m1")


def kspread(k):
    return np.exp2(np.repeat(np.random.randint(-6, 7, k // 32), 32).astype(np.float64))


B, S, D, H, DH = 2, 256, 1024, 16, 128
ROPE_BASE = 10000.0


def rope_tables():
    inv_freq = 1.0 / (ROPE_BASE ** (f64(np.arange(0, DH, 2)) / DH))
    freqs = f64(np.arange(S))[:, None] * inv_freq[None, :]
    return np.cos(freqs), np.sin(freqs)


def rope_interleaved(t, cos, sin):
    x1 = t[..., 0::2]
    x2 = t[..., 1::2]
    c = cos[None, :, None, :]
    s_ = sin[None, :, None, :]
    even = x1 * c - x2 * s_
    odd = x1 * s_ + x2 * c
    return np.stack((even, odd), axis=-1).reshape(t.shape)


def setup_inputs():
    s = kspread(D)
    x = np.random.standard_normal((B, S, D)) * s
    x_words, x_scales = pack4(np.ascontiguousarray(x.reshape(B * S, D).T))
    w = np.random.standard_normal((2 * H * DH, D)) / np.sqrt(D) / s[None, :]
    words, scales = pack4(np.ascontiguousarray(w.T))
    return {"x_words": x_words, "x_scales": x_scales, "wqk_w_words": words, "wqk_w_scales": scales}


def reference(x_words, x_scales, wqk_w_words, wqk_w_scales):
    xqk = (unpack4(x_words, x_scales).T.reshape(B, S, D) @ unpack4(wqk_w_words, wqk_w_scales)).reshape(B, S, 2, H, DH)
    cos, sin = rope_tables()
    q = rope_interleaved(xqk[:, :, 0], cos, sin).transpose(0, 2, 1, 3)
    k = rope_interleaved(xqk[:, :, 1], cos, sin).transpose(0, 2, 1, 3)
    return q, k

@@ -1,0 +1,289 @@
+import math
+from contextlib import ExitStack
+
+import concourse.mybir as mybir
+from concourse.masks import make_identity
+
+F32 = mybir.dt.float32
+BF16 = mybir.dt.bfloat16
+I32 = mybir.dt.int32
+U8 = mybir.dt.uint8
+FP4X4 = mybir.dt.float4_e2m1fn_x4
+ALU = mybir.AluOpType
+ACT = mybir.ActivationFunctionType
+
+P = 128
+PASSES = 2
+TOKENS = 512
+COLS = 4096
+BLOCK = 512
+HEADS_PER_BLOCK = 4
+PAIRS = 64
+ROPE_BASE = 10000.0
+CHUNKS = ((0, 1), (1, 4), (4, 8))
+SCHEDULE = "NNn'Ntntn'tnNttn'tntnNttttn'NtnNvNNv"
+N_BLOCKS = (0, 2, 4, 6, 7)
+T_BLOCKS = (1, 3, 5)
+LAG = 4
+HOLD = 2
+WARM_UP = 10
+
+FLOPS = 2 * TOKENS * 1024 * COLS
+
+
+def tile_attention_pa_kernel(tc, x_words, x_scales, wqk_w_words, wqk_w_scales, out_0, out_1):
+    nc = tc.nc
+    outs = (out_0, out_1)
+
+    with ExitStack() as ctx:
+        ctx.enter_context(tc.manual_schedule())
+        keep = ctx.enter_context(tc.tile_pool(name="keep", bufs=1))
+        prods = ctx.enter_context(tc.tile_pool(name="prods", bufs=3))
+        rots = ctx.enter_context(tc.tile_pool(name="rots", bufs=4))
+        psum = ctx.enter_context(tc.psum_pool(name="psum", bufs=8))
+
+        def load_codes(dst, words, c0, c1):
+            nc.sync.dma_start(
+                out=dst[:].bitcast(I32),
+                in_=words[:, :, 2 * c0 : 2 * c1].rearrange("g p n -> p g n").bitcast(I32),
+            )
+
+        def load_scales(dst, scales, c0, c1):
+            for quad in range(4):
+                nc.sync.dma_start(
+                    out=dst[32 * quad : 32 * quad + 4, :, :].bitcast(I32),
+                    in_=scales[:, 4 * quad : 4 * quad + 4, c0:c1].rearrange("g r n -> r g n").bitcast(I32),
+                )
+
+        x_codes = keep.tile([P, PASSES, 2 * TOKENS], U8, name="x_codes", align_bytes=64)
+        x_planes = keep.tile([P, PASSES, TOKENS], U8, name="x_planes", align_bytes=64)
+        w_codes = []
+        w_planes = []
+        for ci, (b0, b1) in enumerate(CHUNKS):
+            width = (b1 - b0) * BLOCK
+            w_codes.append(keep.tile([P, PASSES, 2 * width], U8, name="w_codes%d" % ci, align_bytes=64))
+            w_planes.append(keep.tile([P, PASSES, width], U8, name="w_planes%d" % ci, align_bytes=64))
+
+        nc.vector.memset(x_planes[:].bitcast(I32), 0)
+        nc.vector.memset(w_planes[0][:].bitcast(I32), 0)
+        idle = keep.tile([P, BLOCK], BF16, name="idle")
+        nc.vector.memset(idle[:], 0.0)
+        unused = psum.tile([P, BLOCK], F32, name="total", bufs=2)
+        for i in range(WARM_UP):
+            nc.tensor.matmul(out=unused[:], lhsT=idle[:, 0:P], rhs=idle[:], start=True, stop=True)
+
+        load_codes(x_codes, x_words, 0, TOKENS)
+        load_codes(w_codes[0], wqk_w_words, 0, BLOCK)
+        load_scales(x_planes, x_scales, 0, TOKENS)
+        load_scales(w_planes[0], wqk_w_scales, 0, BLOCK)
+
+        pair = keep.tile([P, 4 * PAIRS], F32, name="pair")
+        nc.gpsimd.iota(
+            pair[:], pattern=[[0, 2], [1, PAIRS], [0, 2]], base=0, channel_multiplier=0,
+            allow_small_or_imprecise_dtypes=True,
+        )
+        freq = keep.tile([P, 4 * PAIRS], F32, name="freq")
+        nc.scalar.activation(out=freq[:], in_=pair[:], func=ACT.Exp, scale=-math.log(ROPE_BASE) / PAIRS)
+        pos = keep.tile([P, 2], F32, name="pos")
+        nc.gpsimd.iota(pos[:], pattern=[[P, 2]], base=0, channel_multiplier=1, allow_small_or_imprecise_dtypes=True)
+        turns = keep.tile([P, 2], F32, name="turns")
+        nc.gpsimd.tensor_scalar(
+            out=turns[:], in0=pos[:], scalar1=1.0 / (2.0 * math.pi), scalar2=0.0, op0=ALU.mult, op1=ALU.add
+        )
+        phase = keep.tile([P, 4 * PAIRS], F32, name="phase")
+        nc.gpsimd.iota(
+            phase[:], pattern=[[1, 2], [0, PAIRS], [-1, 2]], base=1, channel_multiplier=0,
+            allow_small_or_imprecise_dtypes=True,
+        )
+        quarter = keep.tile([P, 4 * PAIRS], F32, name="quarter")
+        nc.gpsimd.tensor_scalar(out=quarter[:], in0=phase[:], scalar1=0.25, scalar2=0.0, op0=ALU.mult, op1=ALU.add)
+        zero = keep.tile([P, 1], F32, name="zero")
+        warm = keep.tile([P, 1], F32, name="warm")
+        nc.gpsimd.memset(zero[:], 0.0)
+        nc.scalar.activation(out=warm[:], in_=zero[:], func=ACT.Sin)
+        for ci in range(1, len(CHUNKS)):
+            nc.gpsimd.memset(w_planes[ci][:].bitcast(F32), 0.0)
+        for ci in range(1, len(CHUNKS)):
+            b0, b1 = CHUNKS[ci]
+            load_codes(w_codes[ci], wqk_w_words, b0 * BLOCK, b1 * BLOCK)
+            load_scales(w_planes[ci], wqk_w_scales, b0 * BLOCK, b1 * BLOCK)
+        ident = keep.tile([P, P], F32, name="ident")
+        make_identity(nc, ident[:])
+
+        angle = keep.tile([P, 2, 4 * PAIRS], F32, name="angle")
+        for a in range(2):
+            nc.vector.scalar_tensor_tensor(
+                out=angle[:, a, :], in0=freq[:], scalar=turns[:, a : a + 1], in1=quarter[:],
+                op0=ALU.mult, op1=ALU.add,
+            )
+        whole = keep.tile([P, 2, 4 * PAIRS], I32, name="whole")
+        nc.vector.tensor_copy(out=whole[:], in_=angle[:])
+        frac = keep.tile([P, 2, 4 * PAIRS], F32, name="frac")
+        nc.vector.tensor_tensor(out=frac[:], in0=angle[:], in1=whole[:], op=ALU.subtract)
+        table = keep.tile([P, 2, 4 * PAIRS], F32, name="table")
+        nc.scalar.activation(out=table[:], in_=frac[:], func=ACT.Sin, scale=2.0 * math.pi)
+
+        swap = keep.tile([P, P], F32, name="swap")
+        for q in range(2):
+            nc.gpsimd.tensor_copy(
+                out=swap[:].rearrange("p (i q) -> p i q", q=2)[:, :, q],
+                in_=ident[:].rearrange("p (i q) -> p i q", q=2)[:, :, 1 - q],
+            )
+        byfeat = keep.tile([P, 2, 2, P], F32, name="byfeat")
+        for plane in range(2):
+            for q in range(2):
+                nc.scalar.copy(
+                    out=byfeat[:, :, plane, :].rearrange("p a (i q) -> p a i q", q=2)[:, :, :, q],
+                    in_=table[:].rearrange("p a (q i o) -> p a q i o", q=2, o=2)[:, :, q, :, q if plane == 0 else 1 - q],
+                )
+        table_t = keep.tile([P, 2, 2 * P], F32, name="table_t")
+
+        def turn_table():
+            turned = psum.tile([P, BLOCK], F32, name="total", bufs=2)
+            for plane in range(2):
+                for a in range(2):
+                    c0 = (2 * plane + a) * P
+                    nc.tensor.transpose(turned[:, c0 : c0 + P], byfeat[:, a, plane, :], ident[:])
+            nc.scalar.copy(
+                out=table_t[:].rearrange("p l (t s) -> p l t s", t=4),
+                in_=turned[:].rearrange("p (l s t) -> p l t s", l=2, t=4),
+            )
+
+        shape5 = [P, 2, HEADS_PER_BLOCK, PAIRS, 2]
+        shape_t = [P, 2, 4, 2, PAIRS]
+
+        def w_slices(col0, width):
+            n = col0 // BLOCK
+            ci = [i for i, (b0, b1) in enumerate(CHUNKS) if b0 <= n < b1][0]
+            c0 = col0 - CHUNKS[ci][0] * BLOCK
+            return [
+                (w_codes[ci][:, g, 2 * c0 : 2 * (c0 + width)].bitcast(FP4X4), w_planes[ci][:, g, c0 : c0 + width])
+                for g in range(PASSES)
+            ]
+
+        def x_slices(tok0, width):
+            return [
+                (x_codes[:, g, 2 * tok0 : 2 * (tok0 + width)].bitcast(FP4X4), x_planes[:, g, tok0 : tok0 + width])
+                for g in range(PASSES)
+            ]
+
+        def multiply(stationary, moving):
+            acc = psum.tile([P, BLOCK], F32, name="acc", bufs=6)
+            for g in range(PASSES):
+                nc.tensor.matmul_mx(
+                    out=acc[:], lhsT=stationary[g][0], lhsT_scale=stationary[g][1],
+                    rhs=moving[g][0], rhs_scale=moving[g][1], start=(g == 0), stop=(g == PASSES - 1),
+                )
+            return acc
+
+        def products_n(engine, m, acc, dst):
+            engine.tensor_tensor(
+                out=dst.rearrange("p (q h i o) -> p q h i o", q=2, h=HEADS_PER_BLOCK, o=2),
+                in0=acc[:].rearrange("p (h i q) -> p q h i", h=HEADS_PER_BLOCK, q=2).unsqueeze(4).to_broadcast(shape5),
+                in1=table[:, m % 2, :].rearrange("p (q i o) -> p q i o", q=2, o=2).unsqueeze(2).to_broadcast(shape5),
+                op=ALU.mult,
+            )
+
+        def products_t(engine, acc, dst):
+            engine.tensor_tensor(
+                out=dst.rearrange("p (l t b s) -> p l t b s", l=2, t=4, b=2),
+                in0=acc[:].rearrange("p (b s t) -> p t b s", b=2, t=4).unsqueeze(1).to_broadcast(shape_t),
+                in1=table_t[:].rearrange("p l (t s) -> p l t s", t=4).unsqueeze(3).to_broadcast(shape_t),
+                op=ALU.mult,
+            )
+
+        def store_n(queue, n, m, src):
+            h0 = (n % 4) * HEADS_PER_BLOCK
+            dst = outs[n // 4][m // 2, h0 : h0 + HEADS_PER_BLOCK, P * (m % 2) : P * (m % 2 + 1), :]
+            queue.dma_start(
+                out=dst.rearrange("h p j -> p h j"),
+                in_=src.rearrange("p (h j) -> p h j", h=HEADS_PER_BLOCK),
+            )
+
+        pieces = []
+        for ch in SCHEDULE:
+            if ch == "'":
+                pieces[-1][1] = True
+            else:
+                pieces.append([ch, False])
+        n_list = [(n, m) for n in N_BLOCKS for m in range(4)]
+        t_list = [4 * n + h for n in T_BLOCKS for h in range(4)]
+        assert len([p for p in pieces if p[0] == "t"]) == len(t_list)
+        assert len(pieces) == len(n_list) + len(t_list)
+
+        waiting = {}
+        by_vector = []
+        group = []
+        prod = None
+        n_seen = 0
+        t_seen = 0
+        held = {}
+        for k in range(len(pieces) + LAG + 1):
+            if k < len(pieces):
+                kind, via_gpsimd = pieces[k]
+                if kind == "t":
+                    head = t_list[t_seen]
+                    t_seen += 1
+                    acc = multiply(w_slices(P * head, P), x_slices(0, TOKENS))
+                else:
+                    n, m = n_list[n_seen]
+                    n_seen += 1
+                    acc = multiply(x_slices(P * m, P), w_slices(BLOCK * n, BLOCK))
+                source = acc
+                engine = nc.vector
+                if via_gpsimd:
+                    source = rots.tile([P, BLOCK], F32, name="plain", bufs=3)
+                    nc.scalar.copy(out=source[:], in_=acc[:])
+                    engine = nc.gpsimd
+            if k - LAG in waiting:
+                single, old_head = waiting[k - LAG]
+                total = psum.tile([P, BLOCK], F32, name="total", bufs=2)
+                for tb in range(4):
+                    cols = slice(P * tb, P * (tb + 1))
+                    nc.tensor.matmul(
+                        out=total[:, cols], lhsT=single[:, cols], rhs=ident[:], is_transpose=True, start=True, stop=False
+                    )
+                    nc.tensor.matmul(
+                        out=total[:, cols], lhsT=single[:, BLOCK + P * tb : BLOCK + P * (tb + 1)], rhs=swap[:],
+                        is_transpose=True, start=False, stop=True,
+                    )
+                lone = rots.tile([P, BLOCK], F32, name="lone", bufs=6)
+                nc.scalar.copy(out=lone[:], in_=total[:])
+                for b in range(2):
+                    nc.sync.dma_start(
+                        out=outs[old_head // 16][b, old_head % 16, :, :].rearrange("(s t) j -> s (t j)", t=4),
+                        in_=lone[64 * b : 64 * (b + 1), :],
+                    )
+            for gn, gm, src in held.get(k, []):
+                store_n(nc.sync, gn, gm, src)
+            if k < len(pieces):
+                if kind == "t":
+                    single = prods.tile([P, 2 * BLOCK], F32, name="single", bufs=6)
+                    waiting[k] = (single, head)
+                    products_t(engine, source, single[:])
+                elif kind == "v":
+                    single = prods.tile([P, 2 * BLOCK], F32, name="single", bufs=6)
+                    by_vector.append((single, n, m))
+                    products_n(engine, m, source, single[:])
+                else:
+                    if not group:
+                        rest = [p[0] for p in pieces[k:] if p[0] in "nN"]
+                        prod = prods.tile([P, rest.index("N") + 1, 2 * BLOCK], F32, name="prod", bufs=4)
+                    products_n(engine, m, source, prod[:, len(group), :])
+                    group.append((n, m))
+                if kind == "N":
+                    rot = rots.tile([P, len(group), BLOCK], F32, name="rot", bufs=5)
+                    nc.gpsimd.tensor_tensor(
+                        out=rot[:], in0=prod[:, :, 0:BLOCK], in1=prod[:, :, BLOCK : 2 * BLOCK], op=ALU.add
+                    )
+                    held[k + HOLD] = [(gn, gm, rot[:, s, :]) for s, (gn, gm) in enumerate(group)]
+                    group = []
+                if k == 3:
+                    turn_table()
+            if k == len(pieces) - 1:
+                for single, n, m in by_vector:
+                    lone = rots.tile([P, BLOCK], F32, name="lone", bufs=6)
+                    nc.vector.tensor_tensor(
+                        out=lone[:], in0=single[:, 0:BLOCK], in1=single[:, BLOCK : 2 * BLOCK], op=ALU.add
+                    )
+                    store_n(nc.sync, n, m, lone[:])

@@ -145,12 +145,12 @@ def tile_attention_pa_kernel(tc, x_words, x_scales, wqk_w_words, wqk_w_scales, o
                     c0 = (2 * plane + a) * P
                     nc.tensor.transpose(turned[:, c0 : c0 + P], byfeat[:, a, plane, :], ident[:])
             nc.scalar.copy(
-                out=table_t[:].rearrange("p l (t s) -> p l t s", t=4),
-                in_=turned[:].rearrange("p (l s t) -> p l t s", l=2, t=4),
+                out=table_t[:].rearrange("p l (t s) -> p l t s", t=2),
+                in_=turned[:].rearrange("p (l s t) -> p l t s", l=2, t=2),
             )
 
         shape5 = [P, 2, HEADS_PER_BLOCK, PAIRS, 2]
-        shape_t = [P, 2, 4, 2, PAIRS]
+        shape_t = [P, 2, 2, 2, P]
 
         def w_slices(col0, width):
             n = col0 // BLOCK
@@ -186,9 +186,9 @@ def tile_attention_pa_kernel(tc, x_words, x_scales, wqk_w_words, wqk_w_scales, o
 
         def products_t(engine, acc, dst):
             engine.tensor_tensor(
-                out=dst.rearrange("p (l t b s) -> p l t b s", l=2, t=4, b=2),
-                in0=acc[:].rearrange("p (b s t) -> p t b s", b=2, t=4).unsqueeze(1).to_broadcast(shape_t),
-                in1=table_t[:].rearrange("p l (t s) -> p l t s", t=4).unsqueeze(3).to_broadcast(shape_t),
+                out=dst.rearrange("p (l t b s) -> p l t b s", l=2, t=2, b=2),
+                in0=acc[:].rearrange("p (b s t) -> p t b s", b=2, t=2).unsqueeze(1).to_broadcast(shape_t),
+                in1=table_t[:].rearrange("p l (t s) -> p l t s", t=2).unsqueeze(3).to_broadcast(shape_t),
                 op=ALU.mult,
             )
 
@@ -240,20 +240,20 @@ def tile_attention_pa_kernel(tc, x_words, x_scales, wqk_w_words, wqk_w_scales, o
                 total = psum.tile([P, BLOCK], F32, name="total", bufs=2)
                 for tb in range(4):
                     cols = slice(P * tb, P * (tb + 1))
+                    turned_to = slice(P * (2 * (tb % 2) + tb // 2), P * (2 * (tb % 2) + tb // 2 + 1))
                     nc.tensor.matmul(
-                        out=total[:, cols], lhsT=single[:, cols], rhs=ident[:], is_transpose=True, start=True, stop=False
+                        out=total[:, turned_to], lhsT=single[:, cols], rhs=ident[:], is_transpose=True, start=True, stop=False
                     )
                     nc.tensor.matmul(
-                        out=total[:, cols], lhsT=single[:, BLOCK + P * tb : BLOCK + P * (tb + 1)], rhs=swap[:],
+                        out=total[:, turned_to], lhsT=single[:, BLOCK + P * tb : BLOCK + P * (tb + 1)], rhs=swap[:],
                         is_transpose=True, start=False, stop=True,
                     )
                 lone = rots.tile([P, BLOCK], F32, name="lone", bufs=6)
                 nc.scalar.copy(out=lone[:], in_=total[:])
-                for b in range(2):
-                    nc.sync.dma_start(
-                        out=outs[old_head // 16][b, old_head % 16, :, :].rearrange("(s t) j -> s (t j)", t=4),
-                        in_=lone[64 * b : 64 * (b + 1), :],
-                    )
+                nc.sync.dma_start(
+                    out=outs[old_head // 16][:, old_head % 16, :, :].rearrange("b (s t) j -> s b (t j)", t=2),
+                    in_=lone[:].rearrange("p (b f) -> p b f", b=2),
+                )
             for gn, gm, src in held.get(k, []):
                 store_n(nc.sync, gn, gm, src)
             if k < len(pieces):

@@ -26,7 +26,7 @@ N_BLOCKS = (0, 2, 4, 6, 7)
 T_BLOCKS = (1, 3, 5)
 LAG = 4
 HOLD = 2
-WARM_UP = 10
+WARM_UP = 5
 
 FLOPS = 2 * TOKENS * 1024 * COLS
 
@@ -48,8 +48,8 @@ def tile_attention_pa_kernel(tc, x_words, x_scales, wqk_w_words, wqk_w_scales, o
                 in_=words[:, :, 2 * c0 : 2 * c1].rearrange("g p n -> p g n").bitcast(I32),
             )
 
-        def load_scales(dst, scales, c0, c1):
-            for quad in range(4):
+        def load_scales(dst, scales, c0, c1, quads=(0, 1, 2, 3)):
+            for quad in quads:
                 nc.sync.dma_start(
                     out=dst[32 * quad : 32 * quad + 4, :, :].bitcast(I32),
                     in_=scales[:, 4 * quad : 4 * quad + 4, c0:c1].rearrange("g r n -> r g n").bitcast(I32),
@@ -72,9 +72,10 @@ def tile_attention_pa_kernel(tc, x_words, x_scales, wqk_w_words, wqk_w_scales, o
         for i in range(WARM_UP):
             nc.tensor.matmul(out=unused[:], lhsT=idle[:, 0:P], rhs=idle[:], start=True, stop=True)
 
+        load_scales(x_planes, x_scales, 0, TOKENS, (0, 1))
         load_codes(x_codes, x_words, 0, TOKENS)
         load_codes(w_codes[0], wqk_w_words, 0, BLOCK)
-        load_scales(x_planes, x_scales, 0, TOKENS)
+        load_scales(x_planes, x_scales, 0, TOKENS, (2, 3))
         load_scales(w_planes[0], wqk_w_scales, 0, BLOCK)
 
         pair = keep.tile([P, 4 * PAIRS], F32, name="pair")

@@ -64,10 +64,12 @@ def tile_attention_pa_kernel(tc, x_words, x_scales, wqk_w_words, wqk_w_scales, o
             w_codes.append(keep.tile([P, PASSES, 2 * width], U8, name="w_codes%d" % ci, align_bytes=64))
             w_planes.append(keep.tile([P, PASSES, width], U8, name="w_planes%d" % ci, align_bytes=64))
 
-        nc.vector.memset(x_planes[:].bitcast(I32), 0)
-        nc.vector.memset(w_planes[0][:].bitcast(I32), 0)
+        nc.gpsimd.memset(x_planes[:].bitcast(F32), 0.0)
+        nc.gpsimd.memset(w_planes[0][:].bitcast(F32), 0.0)
+        pos = keep.tile([P, 2], F32, name="pos")
+        nc.gpsimd.iota(pos[:], pattern=[[P, 2]], base=0, channel_multiplier=1, allow_small_or_imprecise_dtypes=True)
         idle = keep.tile([P, BLOCK], BF16, name="idle")
-        nc.vector.memset(idle[:], 0.0)
+        nc.gpsimd.memset(idle[:], 0.0)
         unused = psum.tile([P, BLOCK], F32, name="total", bufs=2)
         for i in range(WARM_UP):
             nc.tensor.matmul(out=unused[:], lhsT=idle[:, 0:P], rhs=idle[:], start=True, stop=True)
@@ -77,31 +79,6 @@ def tile_attention_pa_kernel(tc, x_words, x_scales, wqk_w_words, wqk_w_scales, o
         load_codes(w_codes[0], wqk_w_words, 0, BLOCK)
         load_scales(x_planes, x_scales, 0, TOKENS, (2, 3))
         load_scales(w_planes[0], wqk_w_scales, 0, BLOCK)
-
-        pair = keep.tile([P, 4 * PAIRS], F32, name="pair")
-        nc.gpsimd.iota(
-            pair[:], pattern=[[0, 2], [1, PAIRS], [0, 2]], base=0, channel_multiplier=0,
-            allow_small_or_imprecise_dtypes=True,
-        )
-        freq = keep.tile([P, 4 * PAIRS], F32, name="freq")
-        nc.scalar.activation(out=freq[:], in_=pair[:], func=ACT.Exp, scale=-math.log(ROPE_BASE) / PAIRS)
-        pos = keep.tile([P, 2], F32, name="pos")
-        nc.gpsimd.iota(pos[:], pattern=[[P, 2]], base=0, channel_multiplier=1, allow_small_or_imprecise_dtypes=True)
-        turns = keep.tile([P, 2], F32, name="turns")
-        nc.gpsimd.tensor_scalar(
-            out=turns[:], in0=pos[:], scalar1=1.0 / (2.0 * math.pi), scalar2=0.0, op0=ALU.mult, op1=ALU.add
-        )
-        phase = keep.tile([P, 4 * PAIRS], F32, name="phase")
-        nc.gpsimd.iota(
-            phase[:], pattern=[[1, 2], [0, PAIRS], [-1, 2]], base=1, channel_multiplier=0,
-            allow_small_or_imprecise_dtypes=True,
-        )
-        quarter = keep.tile([P, 4 * PAIRS], F32, name="quarter")
-        nc.gpsimd.tensor_scalar(out=quarter[:], in0=phase[:], scalar1=0.25, scalar2=0.0, op0=ALU.mult, op1=ALU.add)
-        zero = keep.tile([P, 1], F32, name="zero")
-        warm = keep.tile([P, 1], F32, name="warm")
-        nc.gpsimd.memset(zero[:], 0.0)
-        nc.scalar.activation(out=warm[:], in_=zero[:], func=ACT.Sin)
         for ci in range(1, len(CHUNKS)):
             nc.gpsimd.memset(w_planes[ci][:].bitcast(F32), 0.0)
         for ci in range(1, len(CHUNKS)):
@@ -111,18 +88,42 @@ def tile_attention_pa_kernel(tc, x_words, x_scales, wqk_w_words, wqk_w_scales, o
         ident = keep.tile([P, P], F32, name="ident")
         make_identity(nc, ident[:])
 
+        unit = keep.tile([P, 2], F32, name="unit")
+        nc.vector.memset(unit[:], 1.0)
+        warm = keep.tile([P, 2], F32, name="warm")
+        nc.scalar.activation(out=warm[:], in_=unit[:], func=ACT.Sin)
+        freq = keep.tile([P, 2 * PAIRS], F32, name="freq")
+        for d in range(4):
+            nc.vector.tensor_scalar(
+                out=freq[:, 2 * d : 2 * d + 2], in0=unit[:], scalar1=ROPE_BASE ** (-d / PAIRS) / (2.0 * math.pi),
+                scalar2=None, op0=ALU.mult,
+            )
+        quarter = keep.tile([P, 4 * PAIRS], F32, name="quarter")
+        by_qio = quarter[:].rearrange("p (q i o) -> p q i o", q=2, o=2)
+        nc.vector.memset(quarter[:], 0.25)
+        nc.vector.memset(by_qio[:, 0, :, 1], 0.0)
+        nc.vector.memset(by_qio[:, 1, :, 0], 0.5)
+        for have in (4, 16):
+            for d in range(1, 4):
+                nc.vector.tensor_scalar(
+                    out=freq[:, 2 * d * have : 2 * (d + 1) * have], in0=freq[:, 0 : 2 * have],
+                    scalar1=ROPE_BASE ** (-d * have / PAIRS), scalar2=None, op0=ALU.mult,
+                )
         angle = keep.tile([P, 2, 4 * PAIRS], F32, name="angle")
+        whole = keep.tile([P, 2, 4 * PAIRS], I32, name="whole")
+        frac = keep.tile([P, 2, 4 * PAIRS], F32, name="frac")
+        table = keep.tile([P, 2, 4 * PAIRS], F32, name="table")
         for a in range(2):
             nc.vector.scalar_tensor_tensor(
-                out=angle[:, a, :], in0=freq[:], scalar=turns[:, a : a + 1], in1=quarter[:],
-                op0=ALU.mult, op1=ALU.add,
+                out=angle[:, a, :].rearrange("p (q f) -> p q f", q=2),
+                in0=freq[:].unsqueeze(1).to_broadcast([P, 2, 2 * PAIRS]), scalar=pos[:, a : a + 1],
+                in1=quarter[:].rearrange("p (q f) -> p q f", q=2), op0=ALU.mult, op1=ALU.add,
             )
-        whole = keep.tile([P, 2, 4 * PAIRS], I32, name="whole")
-        nc.vector.tensor_copy(out=whole[:], in_=angle[:])
-        frac = keep.tile([P, 2, 4 * PAIRS], F32, name="frac")
-        nc.vector.tensor_tensor(out=frac[:], in0=angle[:], in1=whole[:], op=ALU.subtract)
-        table = keep.tile([P, 2, 4 * PAIRS], F32, name="table")
-        nc.scalar.activation(out=table[:], in_=frac[:], func=ACT.Sin, scale=2.0 * math.pi)
+        for a in range(2):
+            nc.vector.tensor_copy(out=whole[:, a, :], in_=angle[:, a, :])
+        for a in range(2):
+            nc.vector.tensor_tensor(out=frac[:, a, :], in0=angle[:, a, :], in1=whole[:, a, :], op=ALU.subtract)
+            nc.scalar.activation(out=table[:, a, :], in_=frac[:, a, :], func=ACT.Sin, scale=2.0 * math.pi)
 
         swap = keep.tile([P, P], F32, name="swap")
         for q in range(2):

@@ -21,7 +21,7 @@ HEADS_PER_BLOCK = 4
 PAIRS = 64
 ROPE_BASE = 10000.0
 CHUNKS = ((0, 1), (1, 4), (4, 8))
-SCHEDULE = "NNn'Ntntn'tnNttn'tntnNttttn'NtnNvNNv"
+SCHEDULE = "NNn'Ntntn'tnNttn'tntnNttttn'NtnNNvvv"
 N_BLOCKS = (0, 2, 4, 6, 7)
 T_BLOCKS = (1, 3, 5)
 LAG = 4

@@ -21,7 +21,7 @@ HEADS_PER_BLOCK = 4
 PAIRS = 64
 ROPE_BASE = 10000.0
 CHUNKS = ((0, 1), (1, 4), (4, 8))
-SCHEDULE = "NNn'Ntntn'tnNttn'tntnNttttn'NtnNNvvv"
+SCHEDULE = "NNn'N" + "tNtNtNN" + "tN'tNtNN" + "tNtNtNN" + "tNtNtvv"
 N_BLOCKS = (0, 2, 4, 6, 7)
 T_BLOCKS = (1, 3, 5)
 LAG = 4

import math
from contextlib import ExitStack

import concourse.mybir as mybir
from concourse.masks import make_identity

F32 = mybir.dt.float32
BF16 = mybir.dt.bfloat16
I32 = mybir.dt.int32
U8 = mybir.dt.uint8
FP4X4 = mybir.dt.float4_e2m1fn_x4
ALU = mybir.AluOpType
ACT = mybir.ActivationFunctionType

P = 128
PASSES = 2
TOKENS = 512
COLS = 4096
BLOCK = 512
HEADS_PER_BLOCK = 4
PAIRS = 64
ROPE_BASE = 10000.0
CHUNKS = ((0, 1), (1, 4), (4, 8))
SCHEDULE = "NNn'N" + "tNtNtNN" + "tN'tNtNN" + "tNtNtNN" + "tNtNtvv"
N_BLOCKS = (0, 2, 4, 6, 7)
T_BLOCKS = (1, 3, 5)
LAG = 4
HOLD = 2
WARM_UP = 5

FLOPS = 2 * TOKENS * 1024 * COLS


def tile_attention_pa_kernel(tc, x_words, x_scales, wqk_w_words, wqk_w_scales, out_0, out_1):
    nc = tc.nc
    outs = (out_0, out_1)

    with ExitStack() as ctx:
        ctx.enter_context(tc.manual_schedule())
        keep = ctx.enter_context(tc.tile_pool(name="keep", bufs=1))
        prods = ctx.enter_context(tc.tile_pool(name="prods", bufs=3))
        rots = ctx.enter_context(tc.tile_pool(name="rots", bufs=4))
        psum = ctx.enter_context(tc.psum_pool(name="psum", bufs=8))

        def load_codes(dst, words, c0, c1):
            nc.sync.dma_start(
                out=dst[:].bitcast(I32),
                in_=words[:, :, 2 * c0 : 2 * c1].rearrange("g p n -> p g n").bitcast(I32),
            )

        def load_scales(dst, scales, c0, c1, quads=(0, 1, 2, 3)):
            for quad in quads:
                nc.sync.dma_start(
                    out=dst[32 * quad : 32 * quad + 4, :, :].bitcast(I32),
                    in_=scales[:, 4 * quad : 4 * quad + 4, c0:c1].rearrange("g r n -> r g n").bitcast(I32),
                )

        x_codes = keep.tile([P, PASSES, 2 * TOKENS], U8, name="x_codes", align_bytes=64)
        x_planes = keep.tile([P, PASSES, TOKENS], U8, name="x_planes", align_bytes=64)
        w_codes = []
        w_planes = []
        for ci, (b0, b1) in enumerate(CHUNKS):
            width = (b1 - b0) * BLOCK
            w_codes.append(keep.tile([P, PASSES, 2 * width], U8, name="w_codes%d" % ci, align_bytes=64))
            w_planes.append(keep.tile([P, PASSES, width], U8, name="w_planes%d" % ci, align_bytes=64))

        nc.gpsimd.memset(x_planes[:].bitcast(F32), 0.0)
        nc.gpsimd.memset(w_planes[0][:].bitcast(F32), 0.0)
        pos = keep.tile([P, 2], F32, name="pos")
        nc.gpsimd.iota(pos[:], pattern=[[P, 2]], base=0, channel_multiplier=1, allow_small_or_imprecise_dtypes=True)
        idle = keep.tile([P, BLOCK], BF16, name="idle")
        nc.gpsimd.memset(idle[:], 0.0)
        unused = psum.tile([P, BLOCK], F32, name="total", bufs=2)
        for i in range(WARM_UP):
            nc.tensor.matmul(out=unused[:], lhsT=idle[:, 0:P], rhs=idle[:], start=True, stop=True)

        load_scales(x_planes, x_scales, 0, TOKENS, (0, 1))
        load_codes(x_codes, x_words, 0, TOKENS)
        load_codes(w_codes[0], wqk_w_words, 0, BLOCK)
        load_scales(x_planes, x_scales, 0, TOKENS, (2, 3))
        load_scales(w_planes[0], wqk_w_scales, 0, BLOCK)
        for ci in range(1, len(CHUNKS)):
            nc.gpsimd.memset(w_planes[ci][:].bitcast(F32), 0.0)
        for ci in range(1, len(CHUNKS)):
            b0, b1 = CHUNKS[ci]
            load_codes(w_codes[ci], wqk_w_words, b0 * BLOCK, b1 * BLOCK)
            load_scales(w_planes[ci], wqk_w_scales, b0 * BLOCK, b1 * BLOCK)
        ident = keep.tile([P, P], F32, name="ident")
        make_identity(nc, ident[:])

        unit = keep.tile([P, 2], F32, name="unit")
        nc.vector.memset(unit[:], 1.0)
        warm = keep.tile([P, 2], F32, name="warm")
        nc.scalar.activation(out=warm[:], in_=unit[:], func=ACT.Sin)
        freq = keep.tile([P, 2 * PAIRS], F32, name="freq")
        for d in range(4):
            nc.vector.tensor_scalar(
                out=freq[:, 2 * d : 2 * d + 2], in0=unit[:], scalar1=ROPE_BASE ** (-d / PAIRS) / (2.0 * math.pi),
                scalar2=None, op0=ALU.mult,
            )
        quarter = keep.tile([P, 4 * PAIRS], F32, name="quarter")
        by_qio = quarter[:].rearrange("p (q i o) -> p q i o", q=2, o=2)
        nc.vector.memset(quarter[:], 0.25)
        nc.vector.memset(by_qio[:, 0, :, 1], 0.0)
        nc.vector.memset(by_qio[:, 1, :, 0], 0.5)
        for have in (4, 16):
            for d in range(1, 4):
                nc.vector.tensor_scalar(
                    out=freq[:, 2 * d * have : 2 * (d + 1) * have], in0=freq[:, 0 : 2 * have],
                    scalar1=ROPE_BASE ** (-d * have / PAIRS), scalar2=None, op0=ALU.mult,
                )
        angle = keep.tile([P, 2, 4 * PAIRS], F32, name="angle")
        whole = keep.tile([P, 2, 4 * PAIRS], I32, name="whole")
        frac = keep.tile([P, 2, 4 * PAIRS], F32, name="frac")
        table = keep.tile([P, 2, 4 * PAIRS], F32, name="table")
        for a in range(2):
            nc.vector.scalar_tensor_tensor(
                out=angle[:, a, :].rearrange("p (q f) -> p q f", q=2),
                in0=freq[:].unsqueeze(1).to_broadcast([P, 2, 2 * PAIRS]), scalar=pos[:, a : a + 1],
                in1=quarter[:].rearrange("p (q f) -> p q f", q=2), op0=ALU.mult, op1=ALU.add,
            )
        for a in range(2):
            nc.vector.tensor_copy(out=whole[:, a, :], in_=angle[:, a, :])
        for a in range(2):
            nc.vector.tensor_tensor(out=frac[:, a, :], in0=angle[:, a, :], in1=whole[:, a, :], op=ALU.subtract)
            nc.scalar.activation(out=table[:, a, :], in_=frac[:, a, :], func=ACT.Sin, scale=2.0 * math.pi)

        swap = keep.tile([P, P], F32, name="swap")
        for q in range(2):
            nc.gpsimd.tensor_copy(
                out=swap[:].rearrange("p (i q) -> p i q", q=2)[:, :, q],
                in_=ident[:].rearrange("p (i q) -> p i q", q=2)[:, :, 1 - q],
            )
        byfeat = keep.tile([P, 2, 2, P], F32, name="byfeat")
        for plane in range(2):
            for q in range(2):
                nc.scalar.copy(
                    out=byfeat[:, :, plane, :].rearrange("p a (i q) -> p a i q", q=2)[:, :, :, q],
                    in_=table[:].rearrange("p a (q i o) -> p a q i o", q=2, o=2)[:, :, q, :, q if plane == 0 else 1 - q],
                )
        table_t = keep.tile([P, 2, 2 * P], F32, name="table_t")

        def turn_table():
            turned = psum.tile([P, BLOCK], F32, name="total", bufs=2)
            for plane in range(2):
                for a in range(2):
                    c0 = (2 * plane + a) * P
                    nc.tensor.transpose(turned[:, c0 : c0 + P], byfeat[:, a, plane, :], ident[:])
            nc.scalar.copy(
                out=table_t[:].rearrange("p l (t s) -> p l t s", t=2),
                in_=turned[:].rearrange("p (l s t) -> p l t s", l=2, t=2),
            )

        shape5 = [P, 2, HEADS_PER_BLOCK, PAIRS, 2]
        shape_t = [P, 2, 2, 2, P]

        def w_slices(col0, width):
            n = col0 // BLOCK
            ci = [i for i, (b0, b1) in enumerate(CHUNKS) if b0 <= n < b1][0]
            c0 = col0 - CHUNKS[ci][0] * BLOCK
            return [
                (w_codes[ci][:, g, 2 * c0 : 2 * (c0 + width)].bitcast(FP4X4), w_planes[ci][:, g, c0 : c0 + width])
                for g in range(PASSES)
            ]

        def x_slices(tok0, width):
            return [
                (x_codes[:, g, 2 * tok0 : 2 * (tok0 + width)].bitcast(FP4X4), x_planes[:, g, tok0 : tok0 + width])
                for g in range(PASSES)
            ]

        def multiply(stationary, moving):
            acc = psum.tile([P, BLOCK], F32, name="acc", bufs=6)
            for g in range(PASSES):
                nc.tensor.matmul_mx(
                    out=acc[:], lhsT=stationary[g][0], lhsT_scale=stationary[g][1],
                    rhs=moving[g][0], rhs_scale=moving[g][1], start=(g == 0), stop=(g == PASSES - 1),
                )
            return acc

        def products_n(engine, m, acc, dst):
            engine.tensor_tensor(
                out=dst.rearrange("p (q h i o) -> p q h i o", q=2, h=HEADS_PER_BLOCK, o=2),
                in0=acc[:].rearrange("p (h i q) -> p q h i", h=HEADS_PER_BLOCK, q=2).unsqueeze(4).to_broadcast(shape5),
                in1=table[:, m % 2, :].rearrange("p (q i o) -> p q i o", q=2, o=2).unsqueeze(2).to_broadcast(shape5),
                op=ALU.mult,
            )

        def products_t(engine, acc, dst):
            engine.tensor_tensor(
                out=dst.rearrange("p (l t b s) -> p l t b s", l=2, t=2, b=2),
                in0=acc[:].rearrange("p (b s t) -> p t b s", b=2, t=2).unsqueeze(1).to_broadcast(shape_t),
                in1=table_t[:].rearrange("p l (t s) -> p l t s", t=2).unsqueeze(3).to_broadcast(shape_t),
                op=ALU.mult,
            )

        def store_n(queue, n, m, src):
            h0 = (n % 4) * HEADS_PER_BLOCK
            dst = outs[n // 4][m // 2, h0 : h0 + HEADS_PER_BLOCK, P * (m % 2) : P * (m % 2 + 1), :]
            queue.dma_start(
                out=dst.rearrange("h p j -> p h j"),
                in_=src.rearrange("p (h j) -> p h j", h=HEADS_PER_BLOCK),
            )

        pieces = []
        for ch in SCHEDULE:
            if ch == "'":
                pieces[-1][1] = True
            else:
                pieces.append([ch, False])
        n_list = [(n, m) for n in N_BLOCKS for m in range(4)]
        t_list = [4 * n + h for n in T_BLOCKS for h in range(4)]
        assert len([p for p in pieces if p[0] == "t"]) == len(t_list)
        assert len(pieces) == len(n_list) + len(t_list)

        waiting = {}
        by_vector = []
        group = []
        prod = None
        n_seen = 0
        t_seen = 0
        held = {}
        for k in range(len(pieces) + LAG + 1):
            if k < len(pieces):
                kind, via_gpsimd = pieces[k]
                if kind == "t":
                    head = t_list[t_seen]
                    t_seen += 1
                    acc = multiply(w_slices(P * head, P), x_slices(0, TOKENS))
                else:
                    n, m = n_list[n_seen]
                    n_seen += 1
                    acc = multiply(x_slices(P * m, P), w_slices(BLOCK * n, BLOCK))
                source = acc
                engine = nc.vector
                if via_gpsimd:
                    source = rots.tile([P, BLOCK], F32, name="plain", bufs=3)
                    nc.scalar.copy(out=source[:], in_=acc[:])
                    engine = nc.gpsimd
            if k - LAG in waiting:
                single, old_head = waiting[k - LAG]
                total = psum.tile([P, BLOCK], F32, name="total", bufs=2)
                for tb in range(4):
                    cols = slice(P * tb, P * (tb + 1))
                    turned_to = slice(P * (2 * (tb % 2) + tb // 2), P * (2 * (tb % 2) + tb // 2 + 1))
                    nc.tensor.matmul(
                        out=total[:, turned_to], lhsT=single[:, cols], rhs=ident[:], is_transpose=True, start=True, stop=False
                    )
                    nc.tensor.matmul(
                        out=total[:, turned_to], lhsT=single[:, BLOCK + P * tb : BLOCK + P * (tb + 1)], rhs=swap[:],
                        is_transpose=True, start=False, stop=True,
                    )
                lone = rots.tile([P, BLOCK], F32, name="lone", bufs=6)
                nc.scalar.copy(out=lone[:], in_=total[:])
                nc.sync.dma_start(
                    out=outs[old_head // 16][:, old_head % 16, :, :].rearrange("b (s t) j -> s b (t j)", t=2),
                    in_=lone[:].rearrange("p (b f) -> p b f", b=2),
                )
            for gn, gm, src in held.get(k, []):
                store_n(nc.sync, gn, gm, src)
            if k < len(pieces):
                if kind == "t":
                    single = prods.tile([P, 2 * BLOCK], F32, name="single", bufs=6)
                    waiting[k] = (single, head)
                    products_t(engine, source, single[:])
                elif kind == "v":
                    single = prods.tile([P, 2 * BLOCK], F32, name="single", bufs=6)
                    by_vector.append((single, n, m))
                    products_n(engine, m, source, single[:])
                else:
                    if not group:
                        rest = [p[0] for p in pieces[k:] if p[0] in "nN"]
                        prod = prods.tile([P, rest.index("N") + 1, 2 * BLOCK], F32, name="prod", bufs=4)
                    products_n(engine, m, source, prod[:, len(group), :])
                    group.append((n, m))
                if kind == "N":
                    rot = rots.tile([P, len(group), BLOCK], F32, name="rot", bufs=5)
                    nc.gpsimd.tensor_tensor(
                        out=rot[:], in0=prod[:, :, 0:BLOCK], in1=prod[:, :, BLOCK : 2 * BLOCK], op=ALU.add
                    )
                    held[k + HOLD] = [(gn, gm, rot[:, s, :]) for s, (gn, gm) in enumerate(group)]
                    group = []
                if k == 3:
                    turn_table()
            if k == len(pieces) - 1:
                for single, n, m in by_vector:
                    lone = rots.tile([P, BLOCK], F32, name="lone", bufs=6)
                    nc.vector.tensor_tensor(
                        out=lone[:], in0=single[:, 0:BLOCK], in1=single[:, BLOCK : 2 * BLOCK], op=ALU.add
                    )
                    store_n(nc.sync, n, m, lone[:])
